import numpy as np
import ml_dtypes


def mxq(x, axis, fmt="e4m3"):
    dtype, down = {"e4m3": (ml_dtypes.float8_e4m3fn, 7), "e5m2": (ml_dtypes.float8_e5m2, 14)}[fmt]
    v = np.moveaxis(np.asarray(x, np.float32).astype(ml_dtypes.bfloat16).astype(np.float64), axis, -1)
    blocks = v.reshape(v.shape[:-1] + (-1, 32))
    amax = np.abs(blocks).max(-1, keepdims=True)
    byte = np.maximum(np.where(amax > 0, np.frexp(amax)[1] - 1 + 127, 0) - down, 1)
    scale = np.exp2(byte - 127.0)
    codes = (blocks / scale).astype(np.float32).astype(dtype).astype(np.float64)
    return np.moveaxis((codes * scale).reshape(v.shape), -1, axis)


WIDE = False


def mx_kscale(k):
    if not WIDE:
        return np.ones(k)
    levels = np.array([10, -10, 5, -5, 0])
    a = np.random.permutation(np.resize(levels, k // 512 * 4)).reshape(k // 512, 4)
    idx = np.arange(k)
    return np.exp2(a[idx // 512, idx % 128 // 32])


BF16 = ml_dtypes.bfloat16


def bf(x):
    return np.asarray(x, np.float32).astype(BF16)


def f64(x):
    return np.asarray(x).astype(np.float64)


B, N, D, L = 1, 1024, 512, 512
SEGS = N // L


def setup_inputs():
    s = mx_kscale(D)
    col = np.concatenate([np.full(D, np.sqrt(SEGS)), np.ones(D)])
    return {"x": bf(np.random.standard_normal((B, N, D)) * s),
            "w_kv": bf(np.random.standard_normal((D, D + D)) * col / np.sqrt(D) / s[:, None])}


def reference(x, w_kv):
    kv = mxq(f64(x), 2, "e4m3") @ mxq(f64(w_kv), 0, "e4m3")
    k, v = kv[..., :D], kv[..., D:]
    keys_lm = k.reshape(B, L, SEGS, D).mean(axis=2)
    vals_lm = v.reshape(B, L, SEGS, D).mean(axis=2)
    return v, keys_lm, vals_lm

@@ -1,0 +1,151 @@
+from contextlib import ExitStack
+
+import concourse.mybir as mybir
+from concourse.masks import make_identity
+
+F32 = mybir.dt.float32
+BF16 = mybir.dt.bfloat16
+U32 = mybir.dt.uint32
+U8 = mybir.dt.uint8
+FP8X4 = mybir.dt.float8_e4m3fn_x4
+COPY = mybir.ActivationFunctionType.Copy
+
+P = 128
+PACK = 4
+PAIR = 2
+WORDS = PACK // PAIR
+TOKENS = 1024
+D = 512
+SEG = 2
+GROUPS = TOKENS // (P * SEG)
+RUN = 4
+KEYS, VALUES = 0, 1
+
+FLOPS = 2 * TOKENS * D * (2 * D)
+
+
+def tile_ammattention_pa_kernel(tc, x, w_kv, out_0, out_1, out_2):
+    nc = tc.nc
+
+    x_view = x.rearrange("b (p g s) k -> (b p) g (s k)", g=GROUPS, s=SEG)
+    v_view = out_0.rearrange("b (p g s) d -> (b p) g (s d)", g=GROUPS, s=SEG)
+    mean_views = {
+        KEYS: out_1.rearrange("b (p g) d -> (b p) g d", g=GROUPS),
+        VALUES: out_2.rearrange("b (p g) d -> (b p) g d", g=GROUPS),
+    }
+    w_view = w_kv.rearrange("(q t) (h c) -> q h t c", t=PACK, h=2)
+
+    with ExitStack() as ctx:
+        const = ctx.enter_context(tc.tile_pool(name="const", bufs=1))
+        w_pool = ctx.enter_context(tc.tile_pool(name="w", bufs=2))
+        x_pool = ctx.enter_context(tc.tile_pool(name="x", bufs=GROUPS))
+        out_pool = ctx.enter_context(tc.tile_pool(name="out", bufs=GROUPS))
+        xt_psum = ctx.enter_context(tc.psum_pool(name="xt", bufs=2))
+        acc_psum = ctx.enter_context(tc.psum_pool(name="acc", bufs=6))
+
+        def load_w(half):
+            w_raw = w_pool.tile([P, PACK, D], BF16)
+            nc.sync.dma_start(out=w_raw[:], in_=w_view[:, half])
+            return w_raw
+
+        def load_x(g):
+            x_raw = x_pool.tile([P, SEG * D], BF16)
+            nc.sync.dma_start(out=x_raw[:], in_=x_view[:, g])
+            return x_raw
+
+        def quantise_w(w_raw):
+            w_grouped = w_pool.tile([P, D, PACK], BF16, align_bytes=64)
+            nc.vector.tensor_copy(
+                out=w_grouped[:].rearrange("q (c i) t -> q c t i", i=RUN),
+                in_=w_raw[:].rearrange("q t (c i) -> q c t i", i=RUN),
+            )
+            w_codes = w_pool.tile([P, D], U32, align_bytes=64)
+            w_scales = w_pool.tile([P, D], U8, align_bytes=64)
+            nc.vector.quantize_mx(
+                out=w_codes[:].bitcast(FP8X4),
+                scales=w_scales[:],
+                in_=w_grouped[:].rearrange("q c t -> q (c t)"),
+            )
+            return w_codes, w_scales
+
+        def quantise_x(x_raw):
+            words = x_raw[:].bitcast(F32).rearrange(
+                "p (s q u) -> p s u q", s=SEG, u=WORDS
+            )
+            xt = xt_psum.tile([P, SEG, WORDS, P], F32)
+            for s in range(SEG):
+                for u in range(WORDS):
+                    nc.tensor.transpose(xt[:, s, u, :], words[:, s, u, :], identity[:])
+            x_grouped = x_pool.tile([P, SEG * P * PACK], BF16, align_bytes=64)
+            nc.scalar.copy(
+                out=x_grouped[:].bitcast(F32).rearrange(
+                    "q (s p u) -> q s p u", s=SEG, u=WORDS
+                ),
+                in_=xt[:].rearrange("q s u p -> q s p u"),
+            )
+            x_codes = x_pool.tile([P, SEG * P], U32, align_bytes=64)
+            x_scales = x_pool.tile([P, SEG * P], U8, align_bytes=64)
+            nc.vector.quantize_mx(
+                out=x_codes[:].bitcast(FP8X4), scales=x_scales[:], in_=x_grouped[:]
+            )
+            return x_codes, x_scales
+
+        def multiply(acc, x_mx, s, w_mx, start, stop):
+            x_codes, x_scales = x_mx
+            w_codes, w_scales = w_mx
+            tokens = slice(s * P, (s + 1) * P)
+            nc.tensor.matmul_mx(
+                out=acc[:],
+                lhsT=x_codes[:, tokens].bitcast(FP8X4),
+                lhsT_scale=x_scales[:, tokens],
+                rhs=w_codes[:].bitcast(FP8X4),
+                rhs_scale=w_scales[:],
+                start=start,
+                stop=stop,
+            )
+
+        def store_values(g, x_mx, w_mx):
+            v_sb = out_pool.tile([P, SEG, D], F32)
+            for s in range(SEG):
+                acc = acc_psum.tile([P, D], F32, tag="acc")
+                multiply(acc, x_mx, s, w_mx, start=True, stop=True)
+                if s % 2 == 0:
+                    nc.scalar.copy(out=v_sb[:, s, :], in_=acc[:])
+                else:
+                    nc.vector.tensor_copy(out=v_sb[:, s, :], in_=acc[:])
+            nc.sync.dma_start(out=v_view[:, g], in_=v_sb[:].rearrange("p s d -> p (s d)"))
+
+        def store_mean(g, x_mx, w_mx, half):
+            acc = acc_psum.tile([P, D], F32, tag="acc")
+            for s in range(SEG):
+                multiply(acc, x_mx, s, w_mx, start=(s == 0), stop=(s == SEG - 1))
+            mean = out_pool.tile([P, D], F32, tag="mean%d" % half)
+            if half == VALUES or g % 2 == 1:
+                nc.scalar.activation(out=mean[:], in_=acc[:], func=COPY, scale=1.0 / SEG)
+            else:
+                nc.vector.tensor_scalar_mul(out=mean[:], in0=acc[:], scalar1=1.0 / SEG)
+            nc.sync.dma_start(out=mean_views[half][:, g], in_=mean[:])
+
+        w_raw_values = load_w(VALUES)
+        x_raws = [load_x(0)]
+        w_raw_keys = load_w(KEYS)
+        for g in range(1, GROUPS):
+            x_raws.append(load_x(g))
+
+        warm = const.tile([P, 1], F32)
+        nc.vector.memset(warm[:], 0.0)
+        nc.scalar.activation(out=warm[:], in_=warm[:], func=COPY, scale=1.0 / SEG)
+
+        identity = const.tile([P, P], F32)
+        make_identity(nc, identity[:])
+
+        w_values = quantise_w(w_raw_values)
+        x_next = quantise_x(x_raws[0])
+        w_keys = quantise_w(w_raw_keys)
+        for g in range(GROUPS):
+            x_mx = x_next
+            if g + 1 < GROUPS:
+                x_next = quantise_x(x_raws[g + 1])
+            store_values(g, x_mx, w_values)
+            store_mean(g, x_mx, w_values, VALUES)
+            store_mean(g, x_mx, w_keys, KEYS)

@@ -18,7 +18,9 @@ TOKENS = 1024
 D = 512
 SEG = 2
 GROUPS = TOKENS // (P * SEG)
+AHEAD = 2
 RUN = 4
+VECTOR_COLS = 3 * D // 4
 KEYS, VALUES = 0, 1
 
 FLOPS = 2 * TOKENS * D * (2 * D)
@@ -40,8 +42,9 @@ def tile_ammattention_pa_kernel(tc, x, w_kv, out_0, out_1, out_2):
         w_pool = ctx.enter_context(tc.tile_pool(name="w", bufs=2))
         x_pool = ctx.enter_context(tc.tile_pool(name="x", bufs=GROUPS))
         out_pool = ctx.enter_context(tc.tile_pool(name="out", bufs=GROUPS))
-        xt_psum = ctx.enter_context(tc.psum_pool(name="xt", bufs=2))
-        acc_psum = ctx.enter_context(tc.psum_pool(name="acc", bufs=6))
+        xt_psum = ctx.enter_context(tc.psum_pool(name="xt", bufs=AHEAD))
+        acc_psum = ctx.enter_context(tc.psum_pool(name="acc", bufs=8 - AHEAD))
+        ctx.enter_context(tc.manual_schedule())
 
         def load_w(half):
             w_raw = w_pool.tile([P, PACK, D], BF16)
@@ -53,12 +56,19 @@ def tile_ammattention_pa_kernel(tc, x, w_kv, out_0, out_1, out_2):
             nc.sync.dma_start(out=x_raw[:], in_=x_view[:, g])
             return x_raw
 
-        def quantise_w(w_raw):
+        def regroup_w(w_raw):
             w_grouped = w_pool.tile([P, D, PACK], BF16, align_bytes=64)
-            nc.vector.tensor_copy(
-                out=w_grouped[:].rearrange("q (c i) t -> q c t i", i=RUN),
-                in_=w_raw[:].rearrange("q t (c i) -> q c t i", i=RUN),
-            )
+            for copy, cols in (
+                (nc.vector.tensor_copy, slice(0, VECTOR_COLS)),
+                (nc.scalar.copy, slice(VECTOR_COLS, D)),
+            ):
+                copy(
+                    out=w_grouped[:, cols, :].rearrange("q (c i) t -> q c t i", i=RUN),
+                    in_=w_raw[:, :, cols].rearrange("q t (c i) -> q c t i", i=RUN),
+                )
+            return w_grouped
+
+        def quantise_w(w_grouped):
             w_codes = w_pool.tile([P, D], U32, align_bytes=64)
             w_scales = w_pool.tile([P, D], U8, align_bytes=64)
             nc.vector.quantize_mx(
@@ -68,7 +78,7 @@ def tile_ammattention_pa_kernel(tc, x, w_kv, out_0, out_1, out_2):
             )
             return w_codes, w_scales
 
-        def quantise_x(x_raw):
+        def transpose_x(x_raw):
             words = x_raw[:].bitcast(F32).rearrange(
                 "p (s q u) -> p s u q", s=SEG, u=WORDS
             )
@@ -83,6 +93,9 @@ def tile_ammattention_pa_kernel(tc, x, w_kv, out_0, out_1, out_2):
                 ),
                 in_=xt[:].rearrange("q s u p -> q s p u"),
             )
+            return x_grouped
+
+        def quantise_x(x_grouped):
             x_codes = x_pool.tile([P, SEG * P], U32, align_bytes=64)
             x_scales = x_pool.tile([P, SEG * P], U8, align_bytes=64)
             nc.vector.quantize_mx(
@@ -126,11 +139,17 @@ def tile_ammattention_pa_kernel(tc, x, w_kv, out_0, out_1, out_2):
                 nc.vector.tensor_scalar_mul(out=mean[:], in0=acc[:], scalar1=1.0 / SEG)
             nc.sync.dma_start(out=mean_views[half][:, g], in_=mean[:])
 
-        w_raw_values = load_w(VALUES)
+        def values_and_their_means(g):
+            store_values(g, x_mx[g], w_values)
+            store_mean(g, x_mx[g], w_values, VALUES)
+            if g + AHEAD < GROUPS:
+                x_mx.append(quantise_x(transpose_x(x_raws[g + AHEAD])))
+
         x_raws = [load_x(0)]
-        w_raw_keys = load_w(KEYS)
+        w_raw_values = load_w(VALUES)
         for g in range(1, GROUPS):
             x_raws.append(load_x(g))
+        w_raw_keys = load_w(KEYS)
 
         warm = const.tile([P, 1], F32)
         nc.vector.memset(warm[:], 0.0)
@@ -139,13 +158,17 @@ def tile_ammattention_pa_kernel(tc, x, w_kv, out_0, out_1, out_2):
         identity = const.tile([P, P], F32)
         make_identity(nc, identity[:])
 
-        w_values = quantise_w(w_raw_values)
-        x_next = quantise_x(x_raws[0])
-        w_keys = quantise_w(w_raw_keys)
+        x_grouped_first = transpose_x(x_raws[0])
+        w_grouped_values = regroup_w(w_raw_values)
+        x_mx = [quantise_x(x_grouped_first)]
+        w_values = quantise_w(w_grouped_values)
+        for g in range(1, AHEAD):
+            x_mx.append(quantise_x(transpose_x(x_raws[g])))
+
+        for g in range(GROUPS // 2):
+            values_and_their_means(g)
+        w_keys = quantise_w(regroup_w(w_raw_keys))
+        for g in range(GROUPS // 2, GROUPS):
+            values_and_their_means(g)
         for g in range(GROUPS):
-            x_mx = x_next
-            if g + 1 < GROUPS:
-                x_next = quantise_x(x_raws[g + 1])
-            store_values(g, x_mx, w_values)
-            store_mean(g, x_mx, w_values, VALUES)
-            store_mean(g, x_mx, w_keys, KEYS)
+            store_mean(g, x_mx[g], w_keys, KEYS)

@@ -20,8 +20,10 @@ SEG = 2
 GROUPS = TOKENS // (P * SEG)
 AHEAD = 2
 RUN = 4
-VECTOR_COLS = 3 * D // 4
 KEYS, VALUES = 0, 1
+PSUM_BANKS = 8
+XT_BANKS = 3
+WARM_MATMULS = 7
 
 FLOPS = 2 * TOKENS * D * (2 * D)
 
@@ -41,9 +43,10 @@ def tile_ammattention_pa_kernel(tc, x, w_kv, out_0, out_1, out_2):
         const = ctx.enter_context(tc.tile_pool(name="const", bufs=1))
         w_pool = ctx.enter_context(tc.tile_pool(name="w", bufs=2))
         x_pool = ctx.enter_context(tc.tile_pool(name="x", bufs=GROUPS))
+        x_mx_pool = ctx.enter_context(tc.tile_pool(name="x_mx", bufs=GROUPS * SEG))
         out_pool = ctx.enter_context(tc.tile_pool(name="out", bufs=GROUPS))
-        xt_psum = ctx.enter_context(tc.psum_pool(name="xt", bufs=AHEAD))
-        acc_psum = ctx.enter_context(tc.psum_pool(name="acc", bufs=8 - AHEAD))
+        xt_psum = ctx.enter_context(tc.psum_pool(name="xt", bufs=XT_BANKS))
+        acc_psum = ctx.enter_context(tc.psum_pool(name="acc", bufs=PSUM_BANKS - XT_BANKS))
         ctx.enter_context(tc.manual_schedule())
 
         def load_w(half):
@@ -52,20 +55,18 @@ def tile_ammattention_pa_kernel(tc, x, w_kv, out_0, out_1, out_2):
             return w_raw
 
         def load_x(g):
-            x_raw = x_pool.tile([P, SEG * D], BF16)
-            nc.sync.dma_start(out=x_raw[:], in_=x_view[:, g])
+            x_raw = x_pool.tile([P, SEG, D], BF16)
+            nc.sync.dma_start(
+                out=x_raw[:].rearrange("p s k -> p (s k)"), in_=x_view[:, g]
+            )
             return x_raw
 
         def regroup_w(w_raw):
             w_grouped = w_pool.tile([P, D, PACK], BF16, align_bytes=64)
-            for copy, cols in (
-                (nc.vector.tensor_copy, slice(0, VECTOR_COLS)),
-                (nc.scalar.copy, slice(VECTOR_COLS, D)),
-            ):
-                copy(
-                    out=w_grouped[:, cols, :].rearrange("q (c i) t -> q c t i", i=RUN),
-                    in_=w_raw[:, :, cols].rearrange("q t (c i) -> q c t i", i=RUN),
-                )
+            nc.vector.tensor_copy(
+                out=w_grouped[:].rearrange("q (c i) t -> q c t i", i=RUN),
+                in_=w_raw[:].rearrange("q t (c i) -> q c t i", i=RUN),
+            )
             return w_grouped
 
         def quantise_w(w_grouped):
@@ -78,77 +79,63 @@ def tile_ammattention_pa_kernel(tc, x, w_kv, out_0, out_1, out_2):
             )
             return w_codes, w_scales
 
-        def transpose_x(x_raw):
-            words = x_raw[:].bitcast(F32).rearrange(
-                "p (s q u) -> p s u q", s=SEG, u=WORDS
-            )
-            xt = xt_psum.tile([P, SEG, WORDS, P], F32)
-            for s in range(SEG):
-                for u in range(WORDS):
-                    nc.tensor.transpose(xt[:, s, u, :], words[:, s, u, :], identity[:])
-            x_grouped = x_pool.tile([P, SEG * P * PACK], BF16, align_bytes=64)
+        def quantise_x(x_raw, s):
+            words = x_raw[:, s, :].bitcast(F32).rearrange("p (q u) -> p u q", u=WORDS)
+            xt = xt_psum.tile([P, WORDS, P], F32)
+            for u in range(WORDS):
+                nc.tensor.transpose(xt[:, u, :], words[:, u, :], identity[:])
+            x_grouped = x_mx_pool.tile([P, P * PACK], BF16, align_bytes=64)
             nc.scalar.copy(
-                out=x_grouped[:].bitcast(F32).rearrange(
-                    "q (s p u) -> q s p u", s=SEG, u=WORDS
-                ),
-                in_=xt[:].rearrange("q s u p -> q s p u"),
+                out=x_grouped[:].bitcast(F32).rearrange("q (p u) -> q p u", u=WORDS),
+                in_=xt[:].rearrange("q u p -> q p u"),
             )
-            return x_grouped
-
-        def quantise_x(x_grouped):
-            x_codes = x_pool.tile([P, SEG * P], U32, align_bytes=64)
-            x_scales = x_pool.tile([P, SEG * P], U8, align_bytes=64)
+            x_codes = x_mx_pool.tile([P, P], U32, align_bytes=64)
+            x_scales = x_mx_pool.tile([P, P], U8, align_bytes=64)
             nc.vector.quantize_mx(
                 out=x_codes[:].bitcast(FP8X4), scales=x_scales[:], in_=x_grouped[:]
             )
             return x_codes, x_scales
 
-        def multiply(acc, x_mx, s, w_mx, start, stop):
+        def quantise_group(g):
+            return [quantise_x(x_raws[g], s) for s in range(SEG)]
+
+        def multiply(acc, x_mx, w_mx, start, stop):
             x_codes, x_scales = x_mx
             w_codes, w_scales = w_mx
-            tokens = slice(s * P, (s + 1) * P)
             nc.tensor.matmul_mx(
                 out=acc[:],
-                lhsT=x_codes[:, tokens].bitcast(FP8X4),
-                lhsT_scale=x_scales[:, tokens],
+                lhsT=x_codes[:].bitcast(FP8X4),
+                lhsT_scale=x_scales[:],
                 rhs=w_codes[:].bitcast(FP8X4),
                 rhs_scale=w_scales[:],
                 start=start,
                 stop=stop,
             )
 
-        def store_values(g, x_mx, w_mx):
+        def store_values(g):
             v_sb = out_pool.tile([P, SEG, D], F32)
             for s in range(SEG):
                 acc = acc_psum.tile([P, D], F32, tag="acc")
-                multiply(acc, x_mx, s, w_mx, start=True, stop=True)
+                multiply(acc, x_mx[g][s], w_mx[VALUES], start=True, stop=True)
                 if s % 2 == 0:
                     nc.scalar.copy(out=v_sb[:, s, :], in_=acc[:])
                 else:
                     nc.vector.tensor_copy(out=v_sb[:, s, :], in_=acc[:])
             nc.sync.dma_start(out=v_view[:, g], in_=v_sb[:].rearrange("p s d -> p (s d)"))
 
-        def store_mean(g, x_mx, w_mx, half):
+        def store_mean(g, half):
             acc = acc_psum.tile([P, D], F32, tag="acc")
             for s in range(SEG):
-                multiply(acc, x_mx, s, w_mx, start=(s == 0), stop=(s == SEG - 1))
+                multiply(acc, x_mx[g][s], w_mx[half], start=(s == 0), stop=(s == SEG - 1))
             mean = out_pool.tile([P, D], F32, tag="mean%d" % half)
-            if half == VALUES or g % 2 == 1:
+            if (g + half) % 2 == 1:
                 nc.scalar.activation(out=mean[:], in_=acc[:], func=COPY, scale=1.0 / SEG)
             else:
                 nc.vector.tensor_scalar_mul(out=mean[:], in0=acc[:], scalar1=1.0 / SEG)
             nc.sync.dma_start(out=mean_views[half][:, g], in_=mean[:])
 
-        def values_and_their_means(g):
-            store_values(g, x_mx[g], w_values)
-            store_mean(g, x_mx[g], w_values, VALUES)
-            if g + AHEAD < GROUPS:
-                x_mx.append(quantise_x(transpose_x(x_raws[g + AHEAD])))
-
-        x_raws = [load_x(0)]
         w_raw_values = load_w(VALUES)
-        for g in range(1, GROUPS):
-            x_raws.append(load_x(g))
+        x_raws = [load_x(g) for g in range(GROUPS)]
         w_raw_keys = load_w(KEYS)
 
         warm = const.tile([P, 1], F32)
@@ -158,17 +145,23 @@ def tile_ammattention_pa_kernel(tc, x, w_kv, out_0, out_1, out_2):
         identity = const.tile([P, P], F32)
         make_identity(nc, identity[:])
 
-        x_grouped_first = transpose_x(x_raws[0])
-        w_grouped_values = regroup_w(w_raw_values)
-        x_mx = [quantise_x(x_grouped_first)]
-        w_values = quantise_w(w_grouped_values)
-        for g in range(1, AHEAD):
-            x_mx.append(quantise_x(transpose_x(x_raws[g])))
+        unread = acc_psum.tile([P, P], F32, tag="acc")
+        for i in range(WARM_MATMULS):
+            nc.tensor.matmul(
+                out=unread[:], lhsT=identity[:], rhs=identity[:], start=True, stop=True
+            )
 
-        for g in range(GROUPS // 2):
-            values_and_their_means(g)
-        w_keys = quantise_w(regroup_w(w_raw_keys))
-        for g in range(GROUPS // 2, GROUPS):
-            values_and_their_means(g)
+        w_mx = {VALUES: quantise_w(regroup_w(w_raw_values))}
+        x_mx = [quantise_group(g) for g in range(AHEAD)]
+
         for g in range(GROUPS):
-            store_mean(g, x_mx[g], w_keys, KEYS)
+            store_values(g)
+            store_mean(g, VALUES)
+            if g == 0:
+                w_grouped_keys = regroup_w(w_raw_keys)
+            if g + AHEAD < GROUPS:
+                x_mx.append(quantise_group(g + AHEAD))
+            if g + AHEAD == GROUPS:
+                w_mx[KEYS] = quantise_w(w_grouped_keys)
+        for g in range(GROUPS):
+            store_mean(g, KEYS)

@@ -32,26 +32,29 @@ def tile_ammattention_pa_kernel(tc, x, w_kv, out_0, out_1, out_2):
     nc = tc.nc
 
     x_view = x.rearrange("b (p g s) k -> (b p) g (s k)", g=GROUPS, s=SEG)
-    v_view = out_0.rearrange("b (p g s) d -> (b p) g (s d)", g=GROUPS, s=SEG)
+    v_view = out_0.rearrange("b (p g s) d -> (b p) g s d", g=GROUPS, s=SEG)
     mean_views = {
         KEYS: out_1.rearrange("b (p g) d -> (b p) g d", g=GROUPS),
         VALUES: out_2.rearrange("b (p g) d -> (b p) g d", g=GROUPS),
     }
-    w_view = w_kv.rearrange("(q t) (h c) -> q h t c", t=PACK, h=2)
+    w_view = w_kv.rearrange("(u q e) (h c) -> q h u e c", u=WORDS, e=PAIR, h=2)
 
     with ExitStack() as ctx:
         const = ctx.enter_context(tc.tile_pool(name="const", bufs=1))
         w_pool = ctx.enter_context(tc.tile_pool(name="w", bufs=2))
         x_pool = ctx.enter_context(tc.tile_pool(name="x", bufs=GROUPS))
         x_mx_pool = ctx.enter_context(tc.tile_pool(name="x_mx", bufs=GROUPS * SEG))
-        out_pool = ctx.enter_context(tc.tile_pool(name="out", bufs=GROUPS))
+        out_pool = ctx.enter_context(tc.tile_pool(name="out", bufs=GROUPS * SEG))
         xt_psum = ctx.enter_context(tc.psum_pool(name="xt", bufs=XT_BANKS))
         acc_psum = ctx.enter_context(tc.psum_pool(name="acc", bufs=PSUM_BANKS - XT_BANKS))
         ctx.enter_context(tc.manual_schedule())
 
         def load_w(half):
             w_raw = w_pool.tile([P, PACK, D], BF16)
-            nc.sync.dma_start(out=w_raw[:], in_=w_view[:, half])
+            for u in range(WORDS):
+                nc.sync.dma_start(
+                    out=w_raw[:, u * PAIR : (u + 1) * PAIR, :], in_=w_view[:, half, u]
+                )
             return w_raw
 
         def load_x(g):
@@ -61,12 +64,18 @@ def tile_ammattention_pa_kernel(tc, x, w_kv, out_0, out_1, out_2):
             )
             return x_raw
 
-        def regroup_w(w_raw):
+        def regroup_w(w_raw, scalar_cols):
             w_grouped = w_pool.tile([P, D, PACK], BF16, align_bytes=64)
+            cut = D - scalar_cols
             nc.vector.tensor_copy(
-                out=w_grouped[:].rearrange("q (c i) t -> q c t i", i=RUN),
-                in_=w_raw[:].rearrange("q t (c i) -> q c t i", i=RUN),
+                out=w_grouped[:, :cut, :].rearrange("q (c i) t -> q c t i", i=RUN),
+                in_=w_raw[:, :, :cut].rearrange("q t (c i) -> q c t i", i=RUN),
             )
+            if scalar_cols > 0:
+                nc.scalar.copy(
+                    out=w_grouped[:, cut:, :].rearrange("q (c i) t -> q c t i", i=RUN),
+                    in_=w_raw[:, :, cut:].rearrange("q t (c i) -> q c t i", i=RUN),
+                )
             return w_grouped
 
         def quantise_w(w_grouped):
@@ -80,7 +89,7 @@ def tile_ammattention_pa_kernel(tc, x, w_kv, out_0, out_1, out_2):
             return w_codes, w_scales
 
         def quantise_x(x_raw, s):
-            words = x_raw[:, s, :].bitcast(F32).rearrange("p (q u) -> p u q", u=WORDS)
+            words = x_raw[:, s, :].bitcast(F32).rearrange("p (u q) -> p u q", u=WORDS)
             xt = xt_psum.tile([P, WORDS, P], F32)
             for u in range(WORDS):
                 nc.tensor.transpose(xt[:, u, :], words[:, u, :], identity[:])
@@ -113,15 +122,15 @@ def tile_ammattention_pa_kernel(tc, x, w_kv, out_0, out_1, out_2):
             )
 
         def store_values(g):
-            v_sb = out_pool.tile([P, SEG, D], F32)
             for s in range(SEG):
                 acc = acc_psum.tile([P, D], F32, tag="acc")
                 multiply(acc, x_mx[g][s], w_mx[VALUES], start=True, stop=True)
+                v_sb = out_pool.tile([P, D], F32)
                 if s % 2 == 0:
-                    nc.scalar.copy(out=v_sb[:, s, :], in_=acc[:])
+                    nc.scalar.copy(out=v_sb[:], in_=acc[:])
                 else:
-                    nc.vector.tensor_copy(out=v_sb[:, s, :], in_=acc[:])
-            nc.sync.dma_start(out=v_view[:, g], in_=v_sb[:].rearrange("p s d -> p (s d)"))
+                    nc.vector.tensor_copy(out=v_sb[:], in_=acc[:])
+                nc.sync.dma_start(out=v_view[:, g, s], in_=v_sb[:])
 
         def store_mean(g, half):
             acc = acc_psum.tile([P, D], F32, tag="acc")
@@ -151,14 +160,14 @@ def tile_ammattention_pa_kernel(tc, x, w_kv, out_0, out_1, out_2):
                 out=unread[:], lhsT=identity[:], rhs=identity[:], start=True, stop=True
             )
 
-        w_mx = {VALUES: quantise_w(regroup_w(w_raw_values))}
+        w_mx = {VALUES: quantise_w(regroup_w(w_raw_values, scalar_cols=D // 4))}
         x_mx = [quantise_group(g) for g in range(AHEAD)]
 
         for g in range(GROUPS):
             store_values(g)
             store_mean(g, VALUES)
             if g == 0:
-                w_grouped_keys = regroup_w(w_raw_keys)
+                w_grouped_keys = regroup_w(w_raw_keys, scalar_cols=0)
             if g + AHEAD < GROUPS:
                 x_mx.append(quantise_group(g + AHEAD))
             if g + AHEAD == GROUPS:

@@ -18,9 +18,10 @@ TOKENS = 1024
 D = 512
 SEG = 2
 GROUPS = TOKENS // (P * SEG)
+KEYS, VALUES = 0, 1
 AHEAD = 2
 RUN = 4
-KEYS, VALUES = 0, 1
+SCALAR_COLS = D // 4
 PSUM_BANKS = 8
 XT_BANKS = 3
 WARM_MATMULS = 7
@@ -37,24 +38,21 @@ def tile_ammattention_pa_kernel(tc, x, w_kv, out_0, out_1, out_2):
         KEYS: out_1.rearrange("b (p g) d -> (b p) g d", g=GROUPS),
         VALUES: out_2.rearrange("b (p g) d -> (b p) g d", g=GROUPS),
     }
-    w_view = w_kv.rearrange("(u q e) (h c) -> q h u e c", u=WORDS, e=PAIR, h=2)
+    w_view = w_kv.rearrange("(q t) (h c) -> q h t c", t=PACK, h=2)
 
     with ExitStack() as ctx:
         const = ctx.enter_context(tc.tile_pool(name="const", bufs=1))
         w_pool = ctx.enter_context(tc.tile_pool(name="w", bufs=2))
         x_pool = ctx.enter_context(tc.tile_pool(name="x", bufs=GROUPS))
-        x_mx_pool = ctx.enter_context(tc.tile_pool(name="x_mx", bufs=GROUPS * SEG))
-        out_pool = ctx.enter_context(tc.tile_pool(name="out", bufs=GROUPS * SEG))
+        unit_pool = ctx.enter_context(tc.tile_pool(name="unit", bufs=GROUPS * SEG))
+        mean_pool = ctx.enter_context(tc.tile_pool(name="mean", bufs=2 * GROUPS))
         xt_psum = ctx.enter_context(tc.psum_pool(name="xt", bufs=XT_BANKS))
         acc_psum = ctx.enter_context(tc.psum_pool(name="acc", bufs=PSUM_BANKS - XT_BANKS))
         ctx.enter_context(tc.manual_schedule())
 
         def load_w(half):
             w_raw = w_pool.tile([P, PACK, D], BF16)
-            for u in range(WORDS):
-                nc.sync.dma_start(
-                    out=w_raw[:, u * PAIR : (u + 1) * PAIR, :], in_=w_view[:, half, u]
-                )
+            nc.sync.dma_start(out=w_raw[:], in_=w_view[:, half])
             return w_raw
 
         def load_x(g):
@@ -88,29 +86,29 @@ def tile_ammattention_pa_kernel(tc, x, w_kv, out_0, out_1, out_2):
             )
             return w_codes, w_scales
 
-        def quantise_x(x_raw, s):
-            words = x_raw[:, s, :].bitcast(F32).rearrange("p (u q) -> p u q", u=WORDS)
+        def quantise_unit(x_raw, s):
+            words = x_raw[:, s, :].bitcast(F32).rearrange("p (q u) -> p u q", u=WORDS)
             xt = xt_psum.tile([P, WORDS, P], F32)
             for u in range(WORDS):
                 nc.tensor.transpose(xt[:, u, :], words[:, u, :], identity[:])
-            x_grouped = x_mx_pool.tile([P, P * PACK], BF16, align_bytes=64)
+            x_grouped = unit_pool.tile([P, P * PACK], BF16, align_bytes=64)
             nc.scalar.copy(
                 out=x_grouped[:].bitcast(F32).rearrange("q (p u) -> q p u", u=WORDS),
                 in_=xt[:].rearrange("q u p -> q p u"),
             )
-            x_codes = x_mx_pool.tile([P, P], U32, align_bytes=64)
-            x_scales = x_mx_pool.tile([P, P], U8, align_bytes=64)
+            x_codes = unit_pool.tile([P, P], U32, align_bytes=64)
+            x_scales = unit_pool.tile([P, P], U8, align_bytes=64)
             nc.vector.quantize_mx(
                 out=x_codes[:].bitcast(FP8X4), scales=x_scales[:], in_=x_grouped[:]
             )
             return x_codes, x_scales
 
         def quantise_group(g):
-            return [quantise_x(x_raws[g], s) for s in range(SEG)]
+            return [quantise_unit(x_raws[g], s) for s in range(SEG)]
 
-        def multiply(acc, x_mx, w_mx, start, stop):
-            x_codes, x_scales = x_mx
-            w_codes, w_scales = w_mx
+        def multiply(acc, unit, w_half, start, stop):
+            x_codes, x_scales = unit
+            w_codes, w_scales = w_half
             nc.tensor.matmul_mx(
                 out=acc[:],
                 lhsT=x_codes[:].bitcast(FP8X4),
@@ -124,8 +122,8 @@ def tile_ammattention_pa_kernel(tc, x, w_kv, out_0, out_1, out_2):
         def store_values(g):
             for s in range(SEG):
                 acc = acc_psum.tile([P, D], F32, tag="acc")
-                multiply(acc, x_mx[g][s], w_mx[VALUES], start=True, stop=True)
-                v_sb = out_pool.tile([P, D], F32)
+                multiply(acc, units[g][s], w_halves[VALUES], start=True, stop=True)
+                v_sb = unit_pool.tile([P, D], F32)
                 if s % 2 == 0:
                     nc.scalar.copy(out=v_sb[:], in_=acc[:])
                 else:
@@ -135,8 +133,10 @@ def tile_ammattention_pa_kernel(tc, x, w_kv, out_0, out_1, out_2):
         def store_mean(g, half):
             acc = acc_psum.tile([P, D], F32, tag="acc")
             for s in range(SEG):
-                multiply(acc, x_mx[g][s], w_mx[half], start=(s == 0), stop=(s == SEG - 1))
-            mean = out_pool.tile([P, D], F32, tag="mean%d" % half)
+                multiply(
+                    acc, units[g][s], w_halves[half], start=(s == 0), stop=(s == SEG - 1)
+                )
+            mean = mean_pool.tile([P, D], F32)
             if (g + half) % 2 == 1:
                 nc.scalar.activation(out=mean[:], in_=acc[:], func=COPY, scale=1.0 / SEG)
             else:
@@ -147,9 +147,9 @@ def tile_ammattention_pa_kernel(tc, x, w_kv, out_0, out_1, out_2):
         x_raws = [load_x(g) for g in range(GROUPS)]
         w_raw_keys = load_w(KEYS)
 
-        warm = const.tile([P, 1], F32)
-        nc.vector.memset(warm[:], 0.0)
-        nc.scalar.activation(out=warm[:], in_=warm[:], func=COPY, scale=1.0 / SEG)
+        scratch = const.tile([P, 1], F32)
+        nc.vector.memset(scratch[:], 0.0)
+        nc.scalar.activation(out=scratch[:], in_=scratch[:], func=COPY, scale=1.0 / SEG)
 
         identity = const.tile([P, P], F32)
         make_identity(nc, identity[:])
@@ -160,17 +160,17 @@ def tile_ammattention_pa_kernel(tc, x, w_kv, out_0, out_1, out_2):
                 out=unread[:], lhsT=identity[:], rhs=identity[:], start=True, stop=True
             )
 
-        w_mx = {VALUES: quantise_w(regroup_w(w_raw_values, scalar_cols=D // 4))}
-        x_mx = [quantise_group(g) for g in range(AHEAD)]
+        w_halves = {VALUES: quantise_w(regroup_w(w_raw_values, SCALAR_COLS))}
+        units = [quantise_group(g) for g in range(AHEAD)]
 
         for g in range(GROUPS):
             store_values(g)
             store_mean(g, VALUES)
             if g == 0:
-                w_grouped_keys = regroup_w(w_raw_keys, scalar_cols=0)
+                w_grouped_keys = regroup_w(w_raw_keys, 0)
             if g + AHEAD < GROUPS:
-                x_mx.append(quantise_group(g + AHEAD))
+                units.append(quantise_group(g + AHEAD))
             if g + AHEAD == GROUPS:
-                w_mx[KEYS] = quantise_w(w_grouped_keys)
+                w_halves[KEYS] = quantise_w(w_grouped_keys)
         for g in range(GROUPS):
             store_mean(g, KEYS)

from contextlib import ExitStack

import concourse.mybir as mybir
from concourse.masks import make_identity

F32 = mybir.dt.float32
BF16 = mybir.dt.bfloat16
U32 = mybir.dt.uint32
U8 = mybir.dt.uint8
FP8X4 = mybir.dt.float8_e4m3fn_x4
COPY = mybir.ActivationFunctionType.Copy

P = 128
PACK = 4
PAIR = 2
WORDS = PACK // PAIR
TOKENS = 1024
D = 512
SEG = 2
GROUPS = TOKENS // (P * SEG)
KEYS, VALUES = 0, 1
AHEAD = 2
RUN = 4
SCALAR_COLS = D // 4
PSUM_BANKS = 8
XT_BANKS = 3
WARM_MATMULS = 7

FLOPS = 2 * TOKENS * D * (2 * D)


def tile_ammattention_pa_kernel(tc, x, w_kv, out_0, out_1, out_2):
    nc = tc.nc

    x_view = x.rearrange("b (p g s) k -> (b p) g (s k)", g=GROUPS, s=SEG)
    v_view = out_0.rearrange("b (p g s) d -> (b p) g s d", g=GROUPS, s=SEG)
    mean_views = {
        KEYS: out_1.rearrange("b (p g) d -> (b p) g d", g=GROUPS),
        VALUES: out_2.rearrange("b (p g) d -> (b p) g d", g=GROUPS),
    }
    w_view = w_kv.rearrange("(q t) (h c) -> q h t c", t=PACK, h=2)

    with ExitStack() as ctx:
        const = ctx.enter_context(tc.tile_pool(name="const", bufs=1))
        w_pool = ctx.enter_context(tc.tile_pool(name="w", bufs=2))
        x_pool = ctx.enter_context(tc.tile_pool(name="x", bufs=GROUPS))
        unit_pool = ctx.enter_context(tc.tile_pool(name="unit", bufs=GROUPS * SEG))
        mean_pool = ctx.enter_context(tc.tile_pool(name="mean", bufs=2 * GROUPS))
        xt_psum = ctx.enter_context(tc.psum_pool(name="xt", bufs=XT_BANKS))
        acc_psum = ctx.enter_context(tc.psum_pool(name="acc", bufs=PSUM_BANKS - XT_BANKS))
        ctx.enter_context(tc.manual_schedule())

        def load_w(half):
            w_raw = w_pool.tile([P, PACK, D], BF16)
            nc.sync.dma_start(out=w_raw[:], in_=w_view[:, half])
            return w_raw

        def load_x(g):
            x_raw = x_pool.tile([P, SEG, D], BF16)
            nc.sync.dma_start(
                out=x_raw[:].rearrange("p s k -> p (s k)"), in_=x_view[:, g]
            )
            return x_raw

        def regroup_w(w_raw, scalar_cols):
            w_grouped = w_pool.tile([P, D, PACK], BF16, align_bytes=64)
            cut = D - scalar_cols
            nc.vector.tensor_copy(
                out=w_grouped[:, :cut, :].rearrange("q (c i) t -> q c t i", i=RUN),
                in_=w_raw[:, :, :cut].rearrange("q t (c i) -> q c t i", i=RUN),
            )
            if scalar_cols > 0:
                nc.scalar.copy(
                    out=w_grouped[:, cut:, :].rearrange("q (c i) t -> q c t i", i=RUN),
                    in_=w_raw[:, :, cut:].rearrange("q t (c i) -> q c t i", i=RUN),
                )
            return w_grouped

        def quantise_w(w_grouped):
            w_codes = w_pool.tile([P, D], U32, align_bytes=64)
            w_scales = w_pool.tile([P, D], U8, align_bytes=64)
            nc.vector.quantize_mx(
                out=w_codes[:].bitcast(FP8X4),
                scales=w_scales[:],
                in_=w_grouped[:].rearrange("q c t -> q (c t)"),
            )
            return w_codes, w_scales

        def quantise_unit(x_raw, s):
            words = x_raw[:, s, :].bitcast(F32).rearrange("p (q u) -> p u q", u=WORDS)
            xt = xt_psum.tile([P, WORDS, P], F32)
            for u in range(WORDS):
                nc.tensor.transpose(xt[:, u, :], words[:, u, :], identity[:])
            x_grouped = unit_pool.tile([P, P * PACK], BF16, align_bytes=64)
            nc.scalar.copy(
                out=x_grouped[:].bitcast(F32).rearrange("q (p u) -> q p u", u=WORDS),
                in_=xt[:].rearrange("q u p -> q p u"),
            )
            x_codes = unit_pool.tile([P, P], U32, align_bytes=64)
            x_scales = unit_pool.tile([P, P], U8, align_bytes=64)
            nc.vector.quantize_mx(
                out=x_codes[:].bitcast(FP8X4), scales=x_scales[:], in_=x_grouped[:]
            )
            return x_codes, x_scales

        def quantise_group(g):
            return [quantise_unit(x_raws[g], s) for s in range(SEG)]

        def multiply(acc, unit, w_half, start, stop):
            x_codes, x_scales = unit
            w_codes, w_scales = w_half
            nc.tensor.matmul_mx(
                out=acc[:],
                lhsT=x_codes[:].bitcast(FP8X4),
                lhsT_scale=x_scales[:],
                rhs=w_codes[:].bitcast(FP8X4),
                rhs_scale=w_scales[:],
                start=start,
                stop=stop,
            )

        def store_values(g):
            for s in range(SEG):
                acc = acc_psum.tile([P, D], F32, tag="acc")
                multiply(acc, units[g][s], w_halves[VALUES], start=True, stop=True)
                v_sb = unit_pool.tile([P, D], F32)
                if s % 2 == 0:
                    nc.scalar.copy(out=v_sb[:], in_=acc[:])
                else:
                    nc.vector.tensor_copy(out=v_sb[:], in_=acc[:])
                nc.sync.dma_start(out=v_view[:, g, s], in_=v_sb[:])

        def store_mean(g, half):
            acc = acc_psum.tile([P, D], F32, tag="acc")
            for s in range(SEG):
                multiply(
                    acc, units[g][s], w_halves[half], start=(s == 0), stop=(s == SEG - 1)
                )
            mean = mean_pool.tile([P, D], F32)
            if (g + half) % 2 == 1:
                nc.scalar.activation(out=mean[:], in_=acc[:], func=COPY, scale=1.0 / SEG)
            else:
                nc.vector.tensor_scalar_mul(out=mean[:], in0=acc[:], scalar1=1.0 / SEG)
            nc.sync.dma_start(out=mean_views[half][:, g], in_=mean[:])

        w_raw_values = load_w(VALUES)
        x_raws = [load_x(g) for g in range(GROUPS)]
        w_raw_keys = load_w(KEYS)

        scratch = const.tile([P, 1], F32)
        nc.vector.memset(scratch[:], 0.0)
        nc.scalar.activation(out=scratch[:], in_=scratch[:], func=COPY, scale=1.0 / SEG)

        identity = const.tile([P, P], F32)
        make_identity(nc, identity[:])

        unread = acc_psum.tile([P, P], F32, tag="acc")
        for i in range(WARM_MATMULS):
            nc.tensor.matmul(
                out=unread[:], lhsT=identity[:], rhs=identity[:], start=True, stop=True
            )

        w_halves = {VALUES: quantise_w(regroup_w(w_raw_values, SCALAR_COLS))}
        units = [quantise_group(g) for g in range(AHEAD)]

        for g in range(GROUPS):
            store_values(g)
            store_mean(g, VALUES)
            if g == 0:
                w_grouped_keys = regroup_w(w_raw_keys, 0)
            if g + AHEAD < GROUPS:
                units.append(quantise_group(g + AHEAD))
            if g + AHEAD == GROUPS:
                w_halves[KEYS] = quantise_w(w_grouped_keys)
        for g in range(GROUPS):
            store_mean(g, KEYS)
